import numpy as np
import ml_dtypes


def mxq(x, axis, fmt="e4m3"):
    dtype, down = {"e4m3": (ml_dtypes.float8_e4m3fn, 7), "e5m2": (ml_dtypes.float8_e5m2, 14)}[fmt]
    v = np.moveaxis(np.asarray(x, np.float32).astype(ml_dtypes.bfloat16).astype(np.float64), axis, -1)
    blocks = v.reshape(v.shape[:-1] + (-1, 32))
    amax = np.abs(blocks).max(-1, keepdims=True)
    byte = np.maximum(np.where(amax > 0, np.frexp(amax)[1] - 1 + 127, 0) - down, 1)
    scale = np.exp2(byte - 127.0)
    codes = (blocks / scale).astype(np.float32).astype(dtype).astype(np.float64)
    return np.moveaxis((codes * scale).reshape(v.shape), -1, axis)


WIDE = False


def mx_kscale(k):
    if not WIDE:
        return np.ones(k)
    levels = np.array([10, -10, 5, -5, 0])
    a = np.random.permutation(np.resize(levels, k // 512 * 4)).reshape(k // 512, 4)
    idx = np.arange(k)
    return np.exp2(a[idx // 512, idx % 128 // 32])


BF16 = ml_dtypes.bfloat16


def bf(x):
    return np.asarray(x, np.float32).astype(BF16)


def f64(x):
    return np.asarray(x).astype(np.float64)


N1, N2, N3, R1, R = 16, 16, 512, 512, 8192


def setup_inputs():
    s = mx_kscale(R)
    g = R ** (-1.0 / 6.0)
    return {"X": bf(np.random.standard_normal((N1, N2, N3))),
            "A": bf(np.random.standard_normal((N1, R)) * g * s),
            "B": bf(np.random.standard_normal((N2, R)) * g),
            "C": bf(np.random.standard_normal((N3, R)) * g / s)}


def reference(X, A, B, C):
    p = (f64(A)[:, None, :] * f64(B)[None, :, :]).reshape(N1 * N2, R)
    approx = mxq(p, 1, "e4m3") @ mxq(f64(C), 1, "e4m3").T
    return approx.reshape(N1, N2, N3) - f64(X)

@@ -1,0 +1,166 @@
+from contextlib import ExitStack
+
+import concourse.mybir as mybir
+from concourse.masks import make_identity
+
+F32 = mybir.dt.float32
+BF16 = mybir.dt.bfloat16
+U32 = mybir.dt.uint32
+U8 = mybir.dt.uint8
+FP8X4 = mybir.dt.float8_e4m3fn_x4
+
+P = 128
+N1, N2, N3, R = 16, 16, 512, 8192
+PACK = 4
+K_PASS = P * PACK
+PASS_WORDS = K_PASS // 2
+PASSES = R // K_PASS
+ROUND_PASSES = 2
+ROUNDS = PASSES // ROUND_PASSES
+ROUND_R = ROUND_PASSES * K_PASS
+M_TILES = N1 * N2 // P
+M_COLS = N1 * N2
+C_TILES = N3 // P
+SPLIT = P // N1
+
+FLOPS = 2 * N1 * N2 * N3 * R
+
+
+def tile_recon_loss_pa_kernel(tc, X, A, B, C, out):
+    nc = tc.nc
+    with ExitStack() as ctx:
+        keep = ctx.enter_context(tc.tile_pool(name="keep", bufs=1))
+        prod_pool = ctx.enter_context(tc.tile_pool(name="prod", bufs=3))
+        group_pool = ctx.enter_context(tc.tile_pool(name="group", bufs=4))
+        res_pool = ctx.enter_context(tc.tile_pool(name="res", bufs=2))
+        acc_pool = ctx.enter_context(tc.psum_pool(name="acc", bufs=1))
+        turn_pool = ctx.enter_context(tc.psum_pool(name="turn", bufs=6))
+
+        ident = keep.tile([P, P], F32)
+        make_identity(nc, ident[:])
+
+        a_raw = keep.tile([P, R // SPLIT], BF16)
+        nc.sync.dma_start(out=a_raw[:], in_=A.rearrange("i (x w) -> (i x) w", x=SPLIT))
+        b_raw = keep.tile([P, R // SPLIT], BF16)
+        nc.sync.dma_start(out=b_raw[:], in_=B.rearrange("j (x w) -> (j x) w", x=SPLIT))
+        c_view = C.rearrange("(a p) r -> p a r", p=P)
+        c_raw = []
+        for k in range(ROUNDS):
+            c_chunk = keep.tile([P, C_TILES, ROUND_R], BF16, name="c_raw%d" % k)
+            nc.sync.dma_start(out=c_chunk[:], in_=c_view[:, :, k * ROUND_R : (k + 1) * ROUND_R])
+            c_raw.append(c_chunk)
+        x_sb = keep.tile([P, M_TILES, N3], BF16)
+        nc.sync.dma_start(out=x_sb[:], in_=X.rearrange("(h i) j k -> (i j) h k", h=M_TILES))
+
+        def turn_factor(raw, turned, copy):
+            bank = turn_pool.tile([P, 4, P], F32, tag="bank", name="factor_bank")
+            words = raw[:].bitcast(F32)
+            for y in range(4):
+                nc.tensor.transpose(bank[:, y, :], words[:, y * P : (y + 1) * P], ident[:])
+            src = bank[:].rearrange("p (yh u) (i x) -> p yh x i u", u=2, x=SPLIT)
+            dst = turned[:].bitcast(F32).rearrange("p (x yh i u) -> p yh x i u", x=SPLIT, yh=2, u=2)
+            for yh in range(2):
+                copy(out=dst[:, yh], in_=src[:, yh])
+
+        a_t = keep.tile([P, PASSES * N1 * PACK], BF16)
+        b_t = keep.tile([P, PASSES * N2 * PACK], BF16)
+        turn_factor(a_raw, a_t, nc.vector.tensor_copy)
+        turn_factor(b_raw, b_t, nc.scalar.copy)
+        a_by_pass = a_t[:].rearrange("p (g i t) -> p g i t", g=PASSES, i=N1)
+        b_by_pass = b_t[:].rearrange("p (g j t) -> p g j t", g=PASSES, j=N2)
+
+        p_prod = {}
+        p_codes = {}
+        p_scales = {}
+
+        def product(k):
+            passes = slice(k * ROUND_PASSES, (k + 1) * ROUND_PASSES)
+            full = [P, ROUND_PASSES, N1, N2, PACK]
+            prod = prod_pool.tile([P, ROUND_PASSES * M_COLS * PACK], BF16, align_bytes=64, name="prod")
+            nc.vector.tensor_tensor(
+                out=prod[:].rearrange("p (g i j t) -> p g i j t", g=ROUND_PASSES, i=N1, j=N2),
+                in0=a_by_pass[:, passes].unsqueeze(3).to_broadcast(full),
+                in1=b_by_pass[:, passes].unsqueeze(2).to_broadcast(full),
+                op=mybir.AluOpType.mult,
+            )
+            p_prod[k] = prod
+
+        def quantise_p(k):
+            codes = keep.tile([P, ROUND_PASSES * M_COLS], U32, align_bytes=64, name="p_codes%d" % k)
+            scales = keep.tile([P, ROUND_PASSES * M_COLS], U8, align_bytes=64, name="p_scales%d" % k)
+            nc.vector.quantize_mx(out=codes[:].bitcast(FP8X4), scales=scales[:], in_=p_prod[k][:])
+            p_codes[k] = codes
+            p_scales[k] = scales
+
+        c_grouped = {}
+        c_codes = {}
+        c_scales = {}
+
+        def turn_c(k):
+            for g_local in range(ROUND_PASSES):
+                grouped = group_pool.tile([P, N3 * PACK], BF16, align_bytes=64, name="grouped")
+                grouped_words = grouped[:].bitcast(F32)
+                for half in range(2):
+                    bank = turn_pool.tile([P, 2, 2 * P], F32, tag="bank", name="c_bank")
+                    for a in range(2):
+                        words = c_raw[k][:, 2 * half + a, :].bitcast(F32)
+                        for u in range(2):
+                            first = g_local * PASS_WORDS + u * P
+                            nc.tensor.transpose(
+                                bank[:, u, a * P : (a + 1) * P], words[:, first : first + P], ident[:]
+                            )
+                    nc.scalar.copy(
+                        out=grouped_words[:, half * 4 * P : (half + 1) * 4 * P].rearrange(
+                            "p (n u) -> p n u", u=2
+                        ),
+                        in_=bank[:].rearrange("p u n -> p n u"),
+                    )
+                c_grouped[k * ROUND_PASSES + g_local] = grouped
+
+        def quantise_c(g):
+            codes = keep.tile([P, N3], U32, align_bytes=64, name="c_codes%d" % g)
+            scales = keep.tile([P, N3], U8, align_bytes=64, name="c_scales%d" % g)
+            nc.vector.quantize_mx(out=codes[:].bitcast(FP8X4), scales=scales[:], in_=c_grouped[g][:])
+            c_codes[g] = codes
+            c_scales[g] = scales
+
+        acc = [acc_pool.tile([P, N3], F32, name="acc%d" % h) for h in range(M_TILES)]
+
+        def multiply(k):
+            for g_local in range(ROUND_PASSES):
+                g = k * ROUND_PASSES + g_local
+                for h in range(M_TILES):
+                    cols = slice(g_local * M_COLS + h * P, g_local * M_COLS + (h + 1) * P)
+                    nc.tensor.matmul_mx(
+                        out=acc[h][:],
+                        lhsT=p_codes[k][:, cols].bitcast(FP8X4),
+                        lhsT_scale=p_scales[k][:, cols],
+                        rhs=c_codes[g][:].bitcast(FP8X4),
+                        rhs_scale=c_scales[g][:],
+                        start=(g == 0),
+                        stop=(g == PASSES - 1),
+                    )
+
+        product(0)
+        product(1)
+        quantise_p(0)
+        turn_c(0)
+        for k in range(1, ROUNDS):
+            turn_c(k)
+            if k + 1 < ROUNDS:
+                product(k + 1)
+            quantise_c(ROUND_PASSES * (k - 1))
+            quantise_p(k)
+            quantise_c(ROUND_PASSES * (k - 1) + 1)
+            multiply(k - 1)
+        quantise_c(PASSES - 2)
+        quantise_c(PASSES - 1)
+        multiply(ROUNDS - 1)
+
+        out_view = out.rearrange("(h i) j k -> h (i j) k", h=M_TILES)
+        for h in range(M_TILES):
+            res = res_pool.tile([P, N3], F32, name="res")
+            nc.vector.tensor_tensor(
+                out=res[:], in0=acc[h][:], in1=x_sb[:, h, :], op=mybir.AluOpType.subtract
+            )
+            nc.sync.dma_start(out=out_view[h], in_=res[:])

@@ -36,6 +36,8 @@ def tile_recon_loss_pa_kernel(tc, X, A, B, C, out):
         acc_pool = ctx.enter_context(tc.psum_pool(name="acc", bufs=1))
         turn_pool = ctx.enter_context(tc.psum_pool(name="turn", bufs=6))
 
+        ctx.enter_context(tc.manual_schedule())
+
         ident = keep.tile([P, P], F32)
         make_identity(nc, ident[:])
 

@@ -18,6 +18,7 @@ PASSES = R // K_PASS
 ROUND_PASSES = 2
 ROUNDS = PASSES // ROUND_PASSES
 ROUND_R = ROUND_PASSES * K_PASS
+TURN_AHEAD = 2
 M_TILES = N1 * N2 // P
 M_COLS = N1 * N2
 C_TILES = N3 // P
@@ -31,7 +32,7 @@ def tile_recon_loss_pa_kernel(tc, X, A, B, C, out):
     with ExitStack() as ctx:
         keep = ctx.enter_context(tc.tile_pool(name="keep", bufs=1))
         prod_pool = ctx.enter_context(tc.tile_pool(name="prod", bufs=3))
-        group_pool = ctx.enter_context(tc.tile_pool(name="group", bufs=4))
+        group_pool = ctx.enter_context(tc.tile_pool(name="group", bufs=ROUND_PASSES * (TURN_AHEAD + 1)))
         res_pool = ctx.enter_context(tc.tile_pool(name="res", bufs=2))
         acc_pool = ctx.enter_context(tc.psum_pool(name="acc", bufs=1))
         turn_pool = ctx.enter_context(tc.psum_pool(name="turn", bufs=6))
@@ -146,18 +147,19 @@ def tile_recon_loss_pa_kernel(tc, X, A, B, C, out):
         product(0)
         product(1)
         quantise_p(0)
-        turn_c(0)
-        for k in range(1, ROUNDS):
-            turn_c(k)
-            if k + 1 < ROUNDS:
-                product(k + 1)
-            quantise_c(ROUND_PASSES * (k - 1))
-            quantise_p(k)
-            quantise_c(ROUND_PASSES * (k - 1) + 1)
-            multiply(k - 1)
-        quantise_c(PASSES - 2)
-        quantise_c(PASSES - 1)
-        multiply(ROUNDS - 1)
+        for s in range(ROUNDS + TURN_AHEAD):
+            if s < ROUNDS:
+                turn_c(s)
+            m = s - TURN_AHEAD
+            if m < 0:
+                continue
+            if m + 2 < ROUNDS:
+                product(m + 2)
+            quantise_c(ROUND_PASSES * m)
+            if m + 1 < ROUNDS:
+                quantise_p(m + 1)
+            quantise_c(ROUND_PASSES * m + 1)
+            multiply(m)
 
         out_view = out.rearrange("(h i) j k -> h (i j) k", h=M_TILES)
         for h in range(M_TILES):

@@ -18,7 +18,9 @@ PASSES = R // K_PASS
 ROUND_PASSES = 2
 ROUNDS = PASSES // ROUND_PASSES
 ROUND_R = ROUND_PASSES * K_PASS
-TURN_AHEAD = 2
+MX_BEHIND = 3
+FIRST_ROUNDS = 2
+OUT_COLS = 256
 M_TILES = N1 * N2 // P
 M_COLS = N1 * N2
 C_TILES = N3 // P
@@ -32,8 +34,8 @@ def tile_recon_loss_pa_kernel(tc, X, A, B, C, out):
     with ExitStack() as ctx:
         keep = ctx.enter_context(tc.tile_pool(name="keep", bufs=1))
         prod_pool = ctx.enter_context(tc.tile_pool(name="prod", bufs=3))
-        group_pool = ctx.enter_context(tc.tile_pool(name="group", bufs=ROUND_PASSES * (TURN_AHEAD + 1)))
-        res_pool = ctx.enter_context(tc.tile_pool(name="res", bufs=2))
+        group_pool = ctx.enter_context(tc.tile_pool(name="group", bufs=6))
+        res_pool = ctx.enter_context(tc.tile_pool(name="res", bufs=4))
         acc_pool = ctx.enter_context(tc.psum_pool(name="acc", bufs=1))
         turn_pool = ctx.enter_context(tc.psum_pool(name="turn", bufs=6))
 
@@ -62,8 +64,9 @@ def tile_recon_loss_pa_kernel(tc, X, A, B, C, out):
                 nc.tensor.transpose(bank[:, y, :], words[:, y * P : (y + 1) * P], ident[:])
             src = bank[:].rearrange("p (yh u) (i x) -> p yh x i u", u=2, x=SPLIT)
             dst = turned[:].bitcast(F32).rearrange("p (x yh i u) -> p yh x i u", x=SPLIT, yh=2, u=2)
-            for yh in range(2):
-                copy(out=dst[:, yh], in_=src[:, yh])
+            for pieces in (slice(0, FIRST_ROUNDS), slice(FIRST_ROUNDS, SPLIT)):
+                for yh in range(2):
+                    copy(out=dst[:, yh, pieces], in_=src[:, yh, pieces])
 
         a_t = keep.tile([P, PASSES * N1 * PACK], BF16)
         b_t = keep.tile([P, PASSES * N2 * PACK], BF16)
@@ -129,42 +132,45 @@ def tile_recon_loss_pa_kernel(tc, X, A, B, C, out):
 
         acc = [acc_pool.tile([P, N3], F32, name="acc%d" % h) for h in range(M_TILES)]
 
-        def multiply(k):
-            for g_local in range(ROUND_PASSES):
-                g = k * ROUND_PASSES + g_local
-                for h in range(M_TILES):
-                    cols = slice(g_local * M_COLS + h * P, g_local * M_COLS + (h + 1) * P)
-                    nc.tensor.matmul_mx(
-                        out=acc[h][:],
-                        lhsT=p_codes[k][:, cols].bitcast(FP8X4),
-                        lhsT_scale=p_scales[k][:, cols],
-                        rhs=c_codes[g][:].bitcast(FP8X4),
-                        rhs_scale=c_scales[g][:],
-                        start=(g == 0),
-                        stop=(g == PASSES - 1),
-                    )
+        def multiply(g):
+            k, g_local = divmod(g, ROUND_PASSES)
+            for h in range(M_TILES):
+                cols = slice(g_local * M_COLS + h * P, g_local * M_COLS + (h + 1) * P)
+                nc.tensor.matmul_mx(
+                    out=acc[h][:],
+                    lhsT=p_codes[k][:, cols].bitcast(FP8X4),
+                    lhsT_scale=p_scales[k][:, cols],
+                    rhs=c_codes[g][:].bitcast(FP8X4),
+                    rhs_scale=c_scales[g][:],
+                    start=(g == 0),
+                    stop=(g == PASSES - 1),
+                )
 
-        product(0)
-        product(1)
+        for k in range(FIRST_ROUNDS):
+            product(k)
         quantise_p(0)
-        for s in range(ROUNDS + TURN_AHEAD):
+        for s in range(ROUNDS + 2):
             if s < ROUNDS:
                 turn_c(s)
-            m = s - TURN_AHEAD
-            if m < 0:
-                continue
-            if m + 2 < ROUNDS:
-                product(m + 2)
-            quantise_c(ROUND_PASSES * m)
-            if m + 1 < ROUNDS:
-                quantise_p(m + 1)
-            quantise_c(ROUND_PASSES * m + 1)
-            multiply(m)
+            m = s - 1
+            if 0 <= m < ROUNDS:
+                if m + FIRST_ROUNDS < ROUNDS:
+                    product(m + FIRST_ROUNDS)
+                quantise_c(ROUND_PASSES * m)
+                if m + 1 < ROUNDS:
+                    quantise_p(m + 1)
+                quantise_c(ROUND_PASSES * m + 1)
+            last_turned = ROUND_PASSES * (s + 1) - 1
+            for g in range(last_turned - MX_BEHIND - 1, last_turned - MX_BEHIND + 1):
+                if 0 <= g < PASSES:
+                    multiply(g)
 
         out_view = out.rearrange("(h i) j k -> h (i j) k", h=M_TILES)
         for h in range(M_TILES):
-            res = res_pool.tile([P, N3], F32, name="res")
-            nc.vector.tensor_tensor(
-                out=res[:], in0=acc[h][:], in1=x_sb[:, h, :], op=mybir.AluOpType.subtract
-            )
-            nc.sync.dma_start(out=out_view[h], in_=res[:])
+            for first in range(0, N3, OUT_COLS):
+                cols = slice(first, first + OUT_COLS)
+                res = res_pool.tile([P, OUT_COLS], F32, name="res")
+                nc.vector.tensor_tensor(
+                    out=res[:], in0=acc[h][:, cols], in1=x_sb[:, h, cols], op=mybir.AluOpType.subtract
+                )
+                nc.sync.dma_start(out=out_view[h][:, cols], in_=res[:])

from contextlib import ExitStack

import concourse.mybir as mybir
from concourse.masks import make_identity

F32 = mybir.dt.float32
BF16 = mybir.dt.bfloat16
U32 = mybir.dt.uint32
U8 = mybir.dt.uint8
FP8X4 = mybir.dt.float8_e4m3fn_x4

P = 128
N1, N2, N3, R = 16, 16, 512, 8192
PACK = 4
K_PASS = P * PACK
PASS_WORDS = K_PASS // 2
PASSES = R // K_PASS
ROUND_PASSES = 2
ROUNDS = PASSES // ROUND_PASSES
ROUND_R = ROUND_PASSES * K_PASS
MX_BEHIND = 3
FIRST_ROUNDS = 2
OUT_COLS = 256
M_TILES = N1 * N2 // P
M_COLS = N1 * N2
C_TILES = N3 // P
SPLIT = P // N1

FLOPS = 2 * N1 * N2 * N3 * R


def tile_recon_loss_pa_kernel(tc, X, A, B, C, out):
    nc = tc.nc
    with ExitStack() as ctx:
        keep = ctx.enter_context(tc.tile_pool(name="keep", bufs=1))
        prod_pool = ctx.enter_context(tc.tile_pool(name="prod", bufs=3))
        group_pool = ctx.enter_context(tc.tile_pool(name="group", bufs=6))
        res_pool = ctx.enter_context(tc.tile_pool(name="res", bufs=4))
        acc_pool = ctx.enter_context(tc.psum_pool(name="acc", bufs=1))
        turn_pool = ctx.enter_context(tc.psum_pool(name="turn", bufs=6))

        ctx.enter_context(tc.manual_schedule())

        ident = keep.tile([P, P], F32)
        make_identity(nc, ident[:])

        a_raw = keep.tile([P, R // SPLIT], BF16)
        nc.sync.dma_start(out=a_raw[:], in_=A.rearrange("i (x w) -> (i x) w", x=SPLIT))
        b_raw = keep.tile([P, R // SPLIT], BF16)
        nc.sync.dma_start(out=b_raw[:], in_=B.rearrange("j (x w) -> (j x) w", x=SPLIT))
        c_view = C.rearrange("(a p) r -> p a r", p=P)
        c_raw = []
        for k in range(ROUNDS):
            c_chunk = keep.tile([P, C_TILES, ROUND_R], BF16, name="c_raw%d" % k)
            nc.sync.dma_start(out=c_chunk[:], in_=c_view[:, :, k * ROUND_R : (k + 1) * ROUND_R])
            c_raw.append(c_chunk)
        x_sb = keep.tile([P, M_TILES, N3], BF16)
        nc.sync.dma_start(out=x_sb[:], in_=X.rearrange("(h i) j k -> (i j) h k", h=M_TILES))

        def turn_factor(raw, turned, copy):
            bank = turn_pool.tile([P, 4, P], F32, tag="bank", name="factor_bank")
            words = raw[:].bitcast(F32)
            for y in range(4):
                nc.tensor.transpose(bank[:, y, :], words[:, y * P : (y + 1) * P], ident[:])
            src = bank[:].rearrange("p (yh u) (i x) -> p yh x i u", u=2, x=SPLIT)
            dst = turned[:].bitcast(F32).rearrange("p (x yh i u) -> p yh x i u", x=SPLIT, yh=2, u=2)
            for pieces in (slice(0, FIRST_ROUNDS), slice(FIRST_ROUNDS, SPLIT)):
                for yh in range(2):
                    copy(out=dst[:, yh, pieces], in_=src[:, yh, pieces])

        a_t = keep.tile([P, PASSES * N1 * PACK], BF16)
        b_t = keep.tile([P, PASSES * N2 * PACK], BF16)
        turn_factor(a_raw, a_t, nc.vector.tensor_copy)
        turn_factor(b_raw, b_t, nc.scalar.copy)
        a_by_pass = a_t[:].rearrange("p (g i t) -> p g i t", g=PASSES, i=N1)
        b_by_pass = b_t[:].rearrange("p (g j t) -> p g j t", g=PASSES, j=N2)

        p_prod = {}
        p_codes = {}
        p_scales = {}

        def product(k):
            passes = slice(k * ROUND_PASSES, (k + 1) * ROUND_PASSES)
            full = [P, ROUND_PASSES, N1, N2, PACK]
            prod = prod_pool.tile([P, ROUND_PASSES * M_COLS * PACK], BF16, align_bytes=64, name="prod")
            nc.vector.tensor_tensor(
                out=prod[:].rearrange("p (g i j t) -> p g i j t", g=ROUND_PASSES, i=N1, j=N2),
                in0=a_by_pass[:, passes].unsqueeze(3).to_broadcast(full),
                in1=b_by_pass[:, passes].unsqueeze(2).to_broadcast(full),
                op=mybir.AluOpType.mult,
            )
            p_prod[k] = prod

        def quantise_p(k):
            codes = keep.tile([P, ROUND_PASSES * M_COLS], U32, align_bytes=64, name="p_codes%d" % k)
            scales = keep.tile([P, ROUND_PASSES * M_COLS], U8, align_bytes=64, name="p_scales%d" % k)
            nc.vector.quantize_mx(out=codes[:].bitcast(FP8X4), scales=scales[:], in_=p_prod[k][:])
            p_codes[k] = codes
            p_scales[k] = scales

        c_grouped = {}
        c_codes = {}
        c_scales = {}

        def turn_c(k):
            for g_local in range(ROUND_PASSES):
                grouped = group_pool.tile([P, N3 * PACK], BF16, align_bytes=64, name="grouped")
                grouped_words = grouped[:].bitcast(F32)
                for half in range(2):
                    bank = turn_pool.tile([P, 2, 2 * P], F32, tag="bank", name="c_bank")
                    for a in range(2):
                        words = c_raw[k][:, 2 * half + a, :].bitcast(F32)
                        for u in range(2):
                            first = g_local * PASS_WORDS + u * P
                            nc.tensor.transpose(
                                bank[:, u, a * P : (a + 1) * P], words[:, first : first + P], ident[:]
                            )
                    nc.scalar.copy(
                        out=grouped_words[:, half * 4 * P : (half + 1) * 4 * P].rearrange(
                            "p (n u) -> p n u", u=2
                        ),
                        in_=bank[:].rearrange("p u n -> p n u"),
                    )
                c_grouped[k * ROUND_PASSES + g_local] = grouped

        def quantise_c(g):
            codes = keep.tile([P, N3], U32, align_bytes=64, name="c_codes%d" % g)
            scales = keep.tile([P, N3], U8, align_bytes=64, name="c_scales%d" % g)
            nc.vector.quantize_mx(out=codes[:].bitcast(FP8X4), scales=scales[:], in_=c_grouped[g][:])
            c_codes[g] = codes
            c_scales[g] = scales

        acc = [acc_pool.tile([P, N3], F32, name="acc%d" % h) for h in range(M_TILES)]

        def multiply(g):
            k, g_local = divmod(g, ROUND_PASSES)
            for h in range(M_TILES):
                cols = slice(g_local * M_COLS + h * P, g_local * M_COLS + (h + 1) * P)
                nc.tensor.matmul_mx(
                    out=acc[h][:],
                    lhsT=p_codes[k][:, cols].bitcast(FP8X4),
                    lhsT_scale=p_scales[k][:, cols],
                    rhs=c_codes[g][:].bitcast(FP8X4),
                    rhs_scale=c_scales[g][:],
                    start=(g == 0),
                    stop=(g == PASSES - 1),
                )

        for k in range(FIRST_ROUNDS):
            product(k)
        quantise_p(0)
        for s in range(ROUNDS + 2):
            if s < ROUNDS:
                turn_c(s)
            m = s - 1
            if 0 <= m < ROUNDS:
                if m + FIRST_ROUNDS < ROUNDS:
                    product(m + FIRST_ROUNDS)
                quantise_c(ROUND_PASSES * m)
                if m + 1 < ROUNDS:
                    quantise_p(m + 1)
                quantise_c(ROUND_PASSES * m + 1)
            last_turned = ROUND_PASSES * (s + 1) - 1
            for g in range(last_turned - MX_BEHIND - 1, last_turned - MX_BEHIND + 1):
                if 0 <= g < PASSES:
                    multiply(g)

        out_view = out.rearrange("(h i) j k -> h (i j) k", h=M_TILES)
        for h in range(M_TILES):
            for first in range(0, N3, OUT_COLS):
                cols = slice(first, first + OUT_COLS)
                res = res_pool.tile([P, OUT_COLS], F32, name="res")
                nc.vector.tensor_tensor(
                    out=res[:], in0=acc[h][:, cols], in1=x_sb[:, h, cols], op=mybir.AluOpType.subtract
                )
                nc.sync.dma_start(out=out_view[h][:, cols], in_=res[:])
